import numpy as np
import ml_dtypes

BF16 = ml_dtypes.bfloat16


def bf(x):
    return np.asarray(x, np.float32).astype(BF16)


def f32(x):
    return np.asarray(x, np.float32)


def f64(x):
    return np.asarray(x).astype(np.float64)


def striped(idx):
    return np.tile(idx.reshape(-1, 16).T, (8, 1))


S, D, M, N = 4096, 128, 128, 2048
EPS, TERMS, LIM = 1e-6, 150, 6.0


def erf(a):
    c = np.clip(a, -LIM, LIM)
    term = c.copy()
    total = c.copy()
    for n in range(1, TERMS):
        term = term * 2.0 * c * c / (2 * n + 1)
        total = total + term
    val = 2.0 / np.sqrt(np.pi) * np.exp(-c * c) * total
    return np.where(np.abs(a) > LIM, np.sign(a), val)


def gelu_erf(v):
    return 0.5 * v * (1.0 + erf(v / np.sqrt(2.0)))


def setup_inputs():
    spread = 0.5 + 1.5 * np.random.random((S, 1))
    shift = np.random.standard_normal((S, 1))
    seqs = bf(spread * np.random.standard_normal((S, D)) + shift)
    ln_gain = f32(1.0 + 0.1 * np.random.standard_normal((D, 1)))
    ln_bias = f32(0.1 * np.random.standard_normal((D, 1)))
    lin_w = bf(np.random.standard_normal((D, M)) / np.sqrt(D))
    lin_b = f32(0.1 * np.random.standard_normal((M, 1)))
    return {"seqs": seqs, "ln_gain": ln_gain, "ln_bias": ln_bias, "lin_w": lin_w, "lin_b": lin_b, "offs": striped(np.random.permutation(S)[:N])}


def reference(seqs, ln_gain, ln_bias, lin_w, lin_b, offs):
    idx = offs[:16].T.reshape(-1)
    x = f64(seqs)
    mu = x.mean(axis=1, keepdims=True)
    var = ((x - mu) ** 2).mean(axis=1, keepdims=True)
    t = (x - mu) / np.sqrt(var + EPS) * f64(ln_gain).T + f64(ln_bias).T
    return gelu_erf(f64(lin_w).T @ t[idx].T + f64(lin_b))

@@ -1,0 +1,88 @@
+import concourse.mybir as mybir
+from concourse.masks import make_identity
+
+BF16, F32, U16 = mybir.dt.bfloat16, mybir.dt.float32, mybir.dt.uint16
+ACT = mybir.ActivationFunctionType
+ALU = mybir.AluOpType
+
+P = 128
+S, D, M, N = 4096, 128, 128, 2048
+EPS = 1e-6
+BLOCKS_PER_CHUNK = 4
+CHUNK = BLOCKS_PER_CHUNK * P
+CHUNKS = S // CHUNK
+PIECE = 512
+PIECES = N // PIECE
+BN_STATS_DIM, BN_AGGR_DIM = 6, 2
+
+FLOPS = 2 * D * M * N
+
+
+def tile_intp_model_kernel(tc, seqs, ln_gain, ln_bias, lin_w, lin_b, offs, out):
+    nc = tc.nc
+    with (
+        tc.tile_pool(name="held", bufs=1) as held,
+        tc.tile_pool(name="rows", bufs=CHUNKS) as rows,
+        tc.tile_pool(name="small", bufs=4) as small,
+        tc.tile_pool(name="work", bufs=3) as work,
+        tc.psum_pool(name="flip", bufs=2) as flip,
+        tc.psum_pool(name="proj", bufs=2) as proj,
+    ):
+        offsets = held.tile([P, N // 16], U16, name="offsets")
+        nc.sync.dma_start(offsets[:], offs)
+
+        seqs_blocks = seqs.rearrange("(b p) d -> p b d", p=P)
+        raw_chunks = []
+        for c in range(CHUNKS):
+            raw = rows.tile([P, BLOCKS_PER_CHUNK, D], BF16, name="raw")
+            queue = nc.sync if c % 2 == 0 else nc.scalar
+            queue.dma_start(raw[:], seqs_blocks[:, c * BLOCKS_PER_CHUNK : (c + 1) * BLOCKS_PER_CHUNK, :])
+            raw_chunks.append(raw)
+
+        weights = held.tile([D, M], BF16, name="weights")
+        nc.gpsimd.dma_start(weights[:], lin_w)
+        gain = held.tile([D, 1], F32, name="gain")
+        nc.gpsimd.dma_start(gain[:], ln_gain)
+        shift = held.tile([D, 1], F32, name="shift")
+        nc.gpsimd.dma_start(shift[:], ln_bias)
+        out_bias = held.tile([M, 1], F32, name="out_bias")
+        nc.gpsimd.dma_start(out_bias[:], lin_b)
+
+        identity = held.tile([P, P], F32, name="identity")
+        make_identity(nc, identity[:])
+        eps = held.tile([P, 1], F32, name="eps")
+        nc.vector.memset(eps[:], EPS)
+
+        table = held.tile([D, S], BF16, name="table")
+
+        for c in range(CHUNKS):
+            raw = raw_chunks[c]
+            stats = small.tile([P, BLOCKS_PER_CHUNK, BN_STATS_DIM], F32, name="stats")
+            mean_var = small.tile([P, BLOCKS_PER_CHUNK, BN_AGGR_DIM], F32, name="mean_var")
+            for k in range(BLOCKS_PER_CHUNK):
+                nc.vector.bn_stats(stats[:, k, :], raw[:, k, :])
+                nc.vector.bn_aggr(mean_var[:, k, :], stats[:, k, :])
+            std = small.tile([P, BLOCKS_PER_CHUNK], F32, name="std")
+            nc.scalar.activation(std[:], mean_var[:, :, 1], ACT.Sqrt, bias=eps[:])
+            rstd = small.tile([P, BLOCKS_PER_CHUNK], F32, name="rstd")
+            nc.vector.reciprocal(rstd[:], std[:])
+            offset = small.tile([P, BLOCKS_PER_CHUNK], F32, name="offset")
+            nc.vector.scalar_tensor_tensor(offset[:], mean_var[:, :, 0], -1.0, rstd[:], ALU.mult, ALU.mult)
+            normed = work.tile([P, BLOCKS_PER_CHUNK, D], F32, name="normed")
+            flipped = flip.tile([D, CHUNK], F32, name="flipped")
+            for k in range(BLOCKS_PER_CHUNK):
+                nc.scalar.activation(
+                    normed[:, k, :], raw[:, k, :], ACT.Identity, bias=offset[:, k : k + 1], scale=rstd[:, k : k + 1]
+                )
+                nc.tensor.transpose(flipped[:, k * P : (k + 1) * P], normed[:, k, :], identity[:])
+            nc.scalar.activation(
+                table[:, c * CHUNK : (c + 1) * CHUNK], flipped[:], ACT.Identity, bias=shift[:], scale=gain[:]
+            )
+
+        for j in range(PIECES):
+            picked = table[:].indirect(offsets[:, j * (PIECE // 16) : (j + 1) * (PIECE // 16)])
+            product = proj.tile([M, PIECE], F32, name="product")
+            nc.tensor.matmul(product[:], weights[:], picked, start=True, stop=True)
+            result = work.tile([M, PIECE], F32, name="result")
+            nc.scalar.activation(result[:], product[:], ACT.Gelu, bias=out_bias[:])
+            nc.sync.dma_start(out[:, j * PIECE : (j + 1) * PIECE], result[:])

@@ -13,7 +13,6 @@ CHUNK = BLOCKS_PER_CHUNK * P
 CHUNKS = S // CHUNK
 PIECE = 512
 PIECES = N // PIECE
-BN_STATS_DIM, BN_AGGR_DIM = 6, 2
 
 FLOPS = 2 * D * M * N
 
@@ -25,64 +24,83 @@ def tile_intp_model_kernel(tc, seqs, ln_gain, ln_bias, lin_w, lin_b, offs, out):
         tc.tile_pool(name="rows", bufs=CHUNKS) as rows,
         tc.tile_pool(name="small", bufs=4) as small,
         tc.tile_pool(name="work", bufs=3) as work,
-        tc.psum_pool(name="flip", bufs=2) as flip,
-        tc.psum_pool(name="proj", bufs=2) as proj,
+        tc.tile_pool(name="done", bufs=PIECES) as done,
+        tc.psum_pool(name="flip", bufs=3) as flip,
+        tc.psum_pool(name="proj", bufs=PIECES) as proj,
     ):
-        offsets = held.tile([P, N // 16], U16, name="offsets")
-        nc.sync.dma_start(offsets[:], offs)
+        identity = held.tile([P, P], F32, name="identity")
+        make_identity(nc, identity[:])
+        eps = held.tile([P, 1], F32, name="eps")
+        nc.vector.memset(eps[:], EPS)
+        unread = held.tile([P, 1], F32, name="unread")
+        nc.scalar.activation(unread[:], eps[:], ACT.Abs_reciprocal_sqrt)
 
         seqs_blocks = seqs.rearrange("(b p) d -> p b d", p=P)
         raw_chunks = []
         for c in range(CHUNKS):
             raw = rows.tile([P, BLOCKS_PER_CHUNK, D], BF16, name="raw")
-            queue = nc.sync if c % 2 == 0 else nc.scalar
-            queue.dma_start(raw[:], seqs_blocks[:, c * BLOCKS_PER_CHUNK : (c + 1) * BLOCKS_PER_CHUNK, :])
+            nc.sync.dma_start(raw[:], seqs_blocks[:, c * BLOCKS_PER_CHUNK : (c + 1) * BLOCKS_PER_CHUNK, :])
             raw_chunks.append(raw)
+        offsets = held.tile([P, N // 16], U16, name="offsets")
+        nc.sync.dma_start(offsets[:], offs)
 
-        weights = held.tile([D, M], BF16, name="weights")
-        nc.gpsimd.dma_start(weights[:], lin_w)
         gain = held.tile([D, 1], F32, name="gain")
-        nc.gpsimd.dma_start(gain[:], ln_gain)
+        nc.scalar.dma_start(gain[:], ln_gain)
         shift = held.tile([D, 1], F32, name="shift")
-        nc.gpsimd.dma_start(shift[:], ln_bias)
+        nc.scalar.dma_start(shift[:], ln_bias)
+        weights = held.tile([D, M], BF16, name="weights")
+        nc.scalar.dma_start(weights[:], lin_w)
         out_bias = held.tile([M, 1], F32, name="out_bias")
-        nc.gpsimd.dma_start(out_bias[:], lin_b)
-
-        identity = held.tile([P, P], F32, name="identity")
-        make_identity(nc, identity[:])
-        eps = held.tile([P, 1], F32, name="eps")
-        nc.vector.memset(eps[:], EPS)
+        nc.scalar.dma_start(out_bias[:], lin_b)
 
         table = held.tile([D, S], BF16, name="table")
 
-        for c in range(CHUNKS):
-            raw = raw_chunks[c]
-            stats = small.tile([P, BLOCKS_PER_CHUNK, BN_STATS_DIM], F32, name="stats")
-            mean_var = small.tile([P, BLOCKS_PER_CHUNK, BN_AGGR_DIM], F32, name="mean_var")
-            for k in range(BLOCKS_PER_CHUNK):
-                nc.vector.bn_stats(stats[:, k, :], raw[:, k, :])
-                nc.vector.bn_aggr(mean_var[:, k, :], stats[:, k, :])
-            std = small.tile([P, BLOCKS_PER_CHUNK], F32, name="std")
-            nc.scalar.activation(std[:], mean_var[:, :, 1], ACT.Sqrt, bias=eps[:])
+        means, rstds, flipped_chunks = {}, {}, {}
+
+        def statistics(c):
+            stats = small.tile([P, BLOCKS_PER_CHUNK, 3], F32, name="stats")
+            for k in range(0, BLOCKS_PER_CHUNK, 2):
+                nc.vector.bn_stats(
+                    stats[:, k : k + 2, :].rearrange("p k t -> p (k t)"),
+                    raw_chunks[c][:, k : k + 2, :].rearrange("p k d -> p d k"),
+                )
             rstd = small.tile([P, BLOCKS_PER_CHUNK], F32, name="rstd")
-            nc.vector.reciprocal(rstd[:], std[:])
-            offset = small.tile([P, BLOCKS_PER_CHUNK], F32, name="offset")
-            nc.vector.scalar_tensor_tensor(offset[:], mean_var[:, :, 0], -1.0, rstd[:], ALU.mult, ALU.mult)
+            nc.scalar.activation(rstd[:], stats[:, :, 2], ACT.Abs_reciprocal_sqrt, bias=eps[:], scale=1.0 / D)
+            means[c], rstds[c] = stats[:, :, 1], rstd
+
+        def normalise_and_flip(c):
             normed = work.tile([P, BLOCKS_PER_CHUNK, D], F32, name="normed")
             flipped = flip.tile([D, CHUNK], F32, name="flipped")
             for k in range(BLOCKS_PER_CHUNK):
-                nc.scalar.activation(
-                    normed[:, k, :], raw[:, k, :], ACT.Identity, bias=offset[:, k : k + 1], scale=rstd[:, k : k + 1]
+                nc.vector.tensor_scalar(
+                    normed[:, k, :], raw_chunks[c][:, k, :], means[c][:, k : k + 1], rstds[c][:, k : k + 1],
+                    ALU.subtract, ALU.mult,
                 )
                 nc.tensor.transpose(flipped[:, k * P : (k + 1) * P], normed[:, k, :], identity[:])
-            nc.scalar.activation(
-                table[:, c * CHUNK : (c + 1) * CHUNK], flipped[:], ACT.Identity, bias=shift[:], scale=gain[:]
-            )
+            flipped_chunks[c] = flipped
+
+        def gain_and_bias(c):
+            columns = table[:, c * CHUNK : (c + 1) * CHUNK]
+            if c < CHUNKS - 1:
+                nc.scalar.activation(columns, flipped_chunks[c][:], ACT.Identity, bias=shift[:], scale=gain[:])
+            else:
+                nc.vector.tensor_scalar(columns, flipped_chunks[c][:], gain[:], shift[:], ALU.mult, ALU.add)
+
+        for step in range(CHUNKS + 2):
+            if step < CHUNKS:
+                statistics(step)
+            if 1 <= step <= CHUNKS:
+                normalise_and_flip(step - 1)
+            if step >= 2:
+                gain_and_bias(step - 2)
+
+        last_by_scalar = (CHUNKS - 1) * CHUNK - 1
+        nc.scalar.activation(unread[:], table[:, last_by_scalar : last_by_scalar + 1], ACT.Gelu)
 
         for j in range(PIECES):
             picked = table[:].indirect(offsets[:, j * (PIECE // 16) : (j + 1) * (PIECE // 16)])
             product = proj.tile([M, PIECE], F32, name="product")
             nc.tensor.matmul(product[:], weights[:], picked, start=True, stop=True)
-            result = work.tile([M, PIECE], F32, name="result")
+            result = done.tile([M, PIECE], F32, name="result")
             nc.scalar.activation(result[:], product[:], ACT.Gelu, bias=out_bias[:])
             nc.sync.dma_start(out[:, j * PIECE : (j + 1) * PIECE], result[:])

@@ -22,8 +22,8 @@ def tile_intp_model_kernel(tc, seqs, ln_gain, ln_bias, lin_w, lin_b, offs, out):
     with (
         tc.tile_pool(name="held", bufs=1) as held,
         tc.tile_pool(name="rows", bufs=CHUNKS) as rows,
-        tc.tile_pool(name="small", bufs=4) as small,
-        tc.tile_pool(name="work", bufs=3) as work,
+        tc.tile_pool(name="small", bufs=8) as small,
+        tc.tile_pool(name="work", bufs=6) as work,
         tc.tile_pool(name="done", bufs=PIECES) as done,
         tc.psum_pool(name="flip", bufs=3) as flip,
         tc.psum_pool(name="proj", bufs=PIECES) as proj,
@@ -55,44 +55,26 @@ def tile_intp_model_kernel(tc, seqs, ln_gain, ln_bias, lin_w, lin_b, offs, out):
 
         table = held.tile([D, S], BF16, name="table")
 
-        means, rstds, flipped_chunks = {}, {}, {}
-
-        def statistics(c):
-            stats = small.tile([P, BLOCKS_PER_CHUNK, 3], F32, name="stats")
-            for k in range(0, BLOCKS_PER_CHUNK, 2):
-                nc.vector.bn_stats(
-                    stats[:, k : k + 2, :].rearrange("p k t -> p (k t)"),
-                    raw_chunks[c][:, k : k + 2, :].rearrange("p k d -> p d k"),
-                )
-            rstd = small.tile([P, BLOCKS_PER_CHUNK], F32, name="rstd")
-            nc.scalar.activation(rstd[:], stats[:, :, 2], ACT.Abs_reciprocal_sqrt, bias=eps[:], scale=1.0 / D)
-            means[c], rstds[c] = stats[:, :, 1], rstd
-
-        def normalise_and_flip(c):
-            normed = work.tile([P, BLOCKS_PER_CHUNK, D], F32, name="normed")
+        for c in range(CHUNKS):
+            raw = raw_chunks[c]
             flipped = flip.tile([D, CHUNK], F32, name="flipped")
-            for k in range(BLOCKS_PER_CHUNK):
-                nc.vector.tensor_scalar(
-                    normed[:, k, :], raw_chunks[c][:, k, :], means[c][:, k : k + 1], rstds[c][:, k : k + 1],
-                    ALU.subtract, ALU.mult,
-                )
-                nc.tensor.transpose(flipped[:, k * P : (k + 1) * P], normed[:, k, :], identity[:])
-            flipped_chunks[c] = flipped
-
-        def gain_and_bias(c):
+            for first in range(0, BLOCKS_PER_CHUNK, 2):
+                pair = raw[:, first : first + 2, :]
+                stats = small.tile([P, 2, 3], F32, name="stats")
+                nc.vector.bn_stats(stats[:].rearrange("p k t -> p (k t)"), pair.rearrange("p k d -> p d k"))
+                rstd = small.tile([P, 2], F32, name="rstd")
+                nc.scalar.activation(rstd[:], stats[:, :, 2], ACT.Abs_reciprocal_sqrt, bias=eps[:], scale=1.0 / D)
+                normed = work.tile([P, 2, D], F32, name="normed")
+                for k in range(2):
+                    nc.vector.tensor_scalar(
+                        normed[:, k, :], pair[:, k, :], stats[:, k, 1:2], rstd[:, k : k + 1], ALU.subtract, ALU.mult
+                    )
+                    nc.tensor.transpose(flipped[:, (first + k) * P : (first + k + 1) * P], normed[:, k, :], identity[:])
             columns = table[:, c * CHUNK : (c + 1) * CHUNK]
             if c < CHUNKS - 1:
-                nc.scalar.activation(columns, flipped_chunks[c][:], ACT.Identity, bias=shift[:], scale=gain[:])
+                nc.scalar.activation(columns, flipped[:], ACT.Identity, bias=shift[:], scale=gain[:])
             else:
-                nc.vector.tensor_scalar(columns, flipped_chunks[c][:], gain[:], shift[:], ALU.mult, ALU.add)
-
-        for step in range(CHUNKS + 2):
-            if step < CHUNKS:
-                statistics(step)
-            if 1 <= step <= CHUNKS:
-                normalise_and_flip(step - 1)
-            if step >= 2:
-                gain_and_bias(step - 2)
+                nc.vector.tensor_scalar(columns, flipped[:], gain[:], shift[:], ALU.mult, ALU.add)
 
         last_by_scalar = (CHUNKS - 1) * CHUNK - 1
         nc.scalar.activation(unread[:], table[:, last_by_scalar : last_by_scalar + 1], ACT.Gelu)

@@ -8,11 +8,16 @@ ALU = mybir.AluOpType
 P = 128
 S, D, M, N = 4096, 128, 128, 2048
 EPS = 1e-6
+BLOCK = P
+PAIR = 2
 BLOCKS_PER_CHUNK = 4
-CHUNK = BLOCKS_PER_CHUNK * P
+CHUNK = BLOCKS_PER_CHUNK * BLOCK
 CHUNKS = S // CHUNK
+PAIRS = S // (PAIR * BLOCK)
+STATS = 3
 PIECE = 512
 PIECES = N // PIECE
+OFFSETS_PER_COLUMN = 16
 
 FLOPS = 2 * D * M * N
 
@@ -22,8 +27,7 @@ def tile_intp_model_kernel(tc, seqs, ln_gain, ln_bias, lin_w, lin_b, offs, out):
     with (
         tc.tile_pool(name="held", bufs=1) as held,
         tc.tile_pool(name="rows", bufs=CHUNKS) as rows,
-        tc.tile_pool(name="small", bufs=8) as small,
-        tc.tile_pool(name="work", bufs=6) as work,
+        tc.tile_pool(name="ahead", bufs=PAIRS // 2) as ahead,
         tc.tile_pool(name="done", bufs=PIECES) as done,
         tc.psum_pool(name="flip", bufs=3) as flip,
         tc.psum_pool(name="proj", bufs=PIECES) as proj,
@@ -41,7 +45,7 @@ def tile_intp_model_kernel(tc, seqs, ln_gain, ln_bias, lin_w, lin_b, offs, out):
             raw = rows.tile([P, BLOCKS_PER_CHUNK, D], BF16, name="raw")
             nc.sync.dma_start(raw[:], seqs_blocks[:, c * BLOCKS_PER_CHUNK : (c + 1) * BLOCKS_PER_CHUNK, :])
             raw_chunks.append(raw)
-        offsets = held.tile([P, N // 16], U16, name="offsets")
+        offsets = held.tile([P, N // OFFSETS_PER_COLUMN], U16, name="offsets")
         nc.sync.dma_start(offsets[:], offs)
 
         gain = held.tile([D, 1], F32, name="gain")
@@ -56,20 +60,21 @@ def tile_intp_model_kernel(tc, seqs, ln_gain, ln_bias, lin_w, lin_b, offs, out):
         table = held.tile([D, S], BF16, name="table")
 
         for c in range(CHUNKS):
-            raw = raw_chunks[c]
             flipped = flip.tile([D, CHUNK], F32, name="flipped")
-            for first in range(0, BLOCKS_PER_CHUNK, 2):
-                pair = raw[:, first : first + 2, :]
-                stats = small.tile([P, 2, 3], F32, name="stats")
+            for first in range(0, BLOCKS_PER_CHUNK, PAIR):
+                pair = raw_chunks[c][:, first : first + PAIR, :]
+                stats = ahead.tile([P, PAIR, STATS], F32, name="stats")
                 nc.vector.bn_stats(stats[:].rearrange("p k t -> p (k t)"), pair.rearrange("p k d -> p d k"))
-                rstd = small.tile([P, 2], F32, name="rstd")
-                nc.scalar.activation(rstd[:], stats[:, :, 2], ACT.Abs_reciprocal_sqrt, bias=eps[:], scale=1.0 / D)
-                normed = work.tile([P, 2, D], F32, name="normed")
-                for k in range(2):
+                mean, count_times_var = stats[:, :, 1], stats[:, :, 2]
+                rstd = ahead.tile([P, PAIR], F32, name="rstd")
+                nc.scalar.activation(rstd[:], count_times_var, ACT.Abs_reciprocal_sqrt, bias=eps[:], scale=1.0 / D)
+                normed = ahead.tile([P, PAIR, D], F32, name="normed")
+                for k in range(PAIR):
                     nc.vector.tensor_scalar(
-                        normed[:, k, :], pair[:, k, :], stats[:, k, 1:2], rstd[:, k : k + 1], ALU.subtract, ALU.mult
+                        normed[:, k, :], pair[:, k, :], mean[:, k : k + 1], rstd[:, k : k + 1], ALU.subtract, ALU.mult
                     )
-                    nc.tensor.transpose(flipped[:, (first + k) * P : (first + k + 1) * P], normed[:, k, :], identity[:])
+                    block = first + k
+                    nc.tensor.transpose(flipped[:, block * BLOCK : (block + 1) * BLOCK], normed[:, k, :], identity[:])
             columns = table[:, c * CHUNK : (c + 1) * CHUNK]
             if c < CHUNKS - 1:
                 nc.scalar.activation(columns, flipped[:], ACT.Identity, bias=shift[:], scale=gain[:])
@@ -79,8 +84,9 @@ def tile_intp_model_kernel(tc, seqs, ln_gain, ln_bias, lin_w, lin_b, offs, out):
         last_by_scalar = (CHUNKS - 1) * CHUNK - 1
         nc.scalar.activation(unread[:], table[:, last_by_scalar : last_by_scalar + 1], ACT.Gelu)
 
+        columns_per_piece = PIECE // OFFSETS_PER_COLUMN
         for j in range(PIECES):
-            picked = table[:].indirect(offsets[:, j * (PIECE // 16) : (j + 1) * (PIECE // 16)])
+            picked = table[:].indirect(offsets[:, j * columns_per_piece : (j + 1) * columns_per_piece])
             product = proj.tile([M, PIECE], F32, name="product")
             nc.tensor.matmul(product[:], weights[:], picked, start=True, stop=True)
             result = done.tile([M, PIECE], F32, name="result")

@@ -14,6 +14,8 @@ BLOCKS_PER_CHUNK = 4
 CHUNK = BLOCKS_PER_CHUNK * BLOCK
 CHUNKS = S // CHUNK
 PAIRS = S // (PAIR * BLOCK)
+PAIRS_PER_CHUNK = BLOCKS_PER_CHUNK // PAIR
+AHEAD = 2 * PAIRS_PER_CHUNK
 STATS = 3
 PIECE = 512
 PIECES = N // PIECE
@@ -27,11 +29,17 @@ def tile_intp_model_kernel(tc, seqs, ln_gain, ln_bias, lin_w, lin_b, offs, out):
     with (
         tc.tile_pool(name="held", bufs=1) as held,
         tc.tile_pool(name="rows", bufs=CHUNKS) as rows,
-        tc.tile_pool(name="ahead", bufs=PAIRS // 2) as ahead,
+        tc.tile_pool(name="ahead", bufs=AHEAD + 2) as ahead,
+        tc.tile_pool(name="turn", bufs=2 * PAIRS_PER_CHUNK) as turn,
         tc.tile_pool(name="done", bufs=PIECES) as done,
         tc.psum_pool(name="flip", bufs=3) as flip,
         tc.psum_pool(name="proj", bufs=PIECES) as proj,
     ):
+        gain = held.tile([D, 1], F32, name="gain")
+        nc.scalar.dma_start(gain[:], ln_gain)
+        shift = held.tile([D, 1], F32, name="shift")
+        nc.scalar.dma_start(shift[:], ln_bias)
+
         identity = held.tile([P, P], F32, name="identity")
         make_identity(nc, identity[:])
         eps = held.tile([P, 1], F32, name="eps")
@@ -45,41 +53,55 @@ def tile_intp_model_kernel(tc, seqs, ln_gain, ln_bias, lin_w, lin_b, offs, out):
             raw = rows.tile([P, BLOCKS_PER_CHUNK, D], BF16, name="raw")
             nc.sync.dma_start(raw[:], seqs_blocks[:, c * BLOCKS_PER_CHUNK : (c + 1) * BLOCKS_PER_CHUNK, :])
             raw_chunks.append(raw)
+        weights = held.tile([D, M], BF16, name="weights")
+        nc.sync.dma_start(weights[:], lin_w)
         offsets = held.tile([P, N // OFFSETS_PER_COLUMN], U16, name="offsets")
         nc.sync.dma_start(offsets[:], offs)
-
-        gain = held.tile([D, 1], F32, name="gain")
-        nc.scalar.dma_start(gain[:], ln_gain)
-        shift = held.tile([D, 1], F32, name="shift")
-        nc.scalar.dma_start(shift[:], ln_bias)
-        weights = held.tile([D, M], BF16, name="weights")
-        nc.scalar.dma_start(weights[:], lin_w)
         out_bias = held.tile([M, 1], F32, name="out_bias")
-        nc.scalar.dma_start(out_bias[:], lin_b)
+        nc.sync.dma_start(out_bias[:], lin_b)
 
         table = held.tile([D, S], BF16, name="table")
 
-        for c in range(CHUNKS):
-            flipped = flip.tile([D, CHUNK], F32, name="flipped")
-            for first in range(0, BLOCKS_PER_CHUNK, PAIR):
-                pair = raw_chunks[c][:, first : first + PAIR, :]
-                stats = ahead.tile([P, PAIR, STATS], F32, name="stats")
-                nc.vector.bn_stats(stats[:].rearrange("p k t -> p (k t)"), pair.rearrange("p k d -> p d k"))
-                mean, count_times_var = stats[:, :, 1], stats[:, :, 2]
-                rstd = ahead.tile([P, PAIR], F32, name="rstd")
-                nc.scalar.activation(rstd[:], count_times_var, ACT.Abs_reciprocal_sqrt, bias=eps[:], scale=1.0 / D)
-                normed = ahead.tile([P, PAIR, D], F32, name="normed")
-                for k in range(PAIR):
-                    nc.vector.tensor_scalar(
-                        normed[:, k, :], pair[:, k, :], mean[:, k : k + 1], rstd[:, k : k + 1], ALU.subtract, ALU.mult
-                    )
-                    block = first + k
-                    nc.tensor.transpose(flipped[:, block * BLOCK : (block + 1) * BLOCK], normed[:, k, :], identity[:])
+        def raw_pair(q):
+            first = (q % PAIRS_PER_CHUNK) * PAIR
+            return raw_chunks[q // PAIRS_PER_CHUNK][:, first : first + PAIR, :]
+
+        means, rstds = {}, {}
+
+        def statistics(q):
+            stats = ahead.tile([P, PAIR, STATS], F32, name="stats")
+            nc.vector.bn_stats(stats[:].rearrange("p k t -> p (k t)"), raw_pair(q).rearrange("p k d -> p d k"))
+            count_times_var = stats[:, :, 2]
+            rstd = ahead.tile([P, PAIR], F32, name="rstd")
+            nc.scalar.activation(rstd[:], count_times_var, ACT.Abs_reciprocal_sqrt, bias=eps[:], scale=1.0 / D)
+            means[q], rstds[q] = stats[:, :, 1], rstd
+
+        def normalise_and_turn(q, flipped):
+            normed = turn.tile([P, PAIR, D], F32, name="normed")
+            for k in range(PAIR):
+                nc.vector.tensor_scalar(
+                    normed[:, k, :], raw_pair(q)[:, k, :], means[q][:, k : k + 1], rstds[q][:, k : k + 1],
+                    ALU.subtract, ALU.mult,
+                )
+                block = (q % PAIRS_PER_CHUNK) * PAIR + k
+                nc.tensor.transpose(flipped[:, block * BLOCK : (block + 1) * BLOCK], normed[:, k, :], identity[:])
+
+        def gain_and_bias(c, flipped):
             columns = table[:, c * CHUNK : (c + 1) * CHUNK]
             if c < CHUNKS - 1:
                 nc.scalar.activation(columns, flipped[:], ACT.Identity, bias=shift[:], scale=gain[:])
             else:
                 nc.vector.tensor_scalar(columns, flipped[:], gain[:], shift[:], ALU.mult, ALU.add)
+
+        for q in range(AHEAD):
+            statistics(q)
+        for c in range(CHUNKS):
+            flipped = flip.tile([D, CHUNK], F32, name="flipped")
+            for q in range(c * PAIRS_PER_CHUNK, (c + 1) * PAIRS_PER_CHUNK):
+                if q + AHEAD < PAIRS:
+                    statistics(q + AHEAD)
+                normalise_and_turn(q, flipped)
+            gain_and_bias(c, flipped)
 
         last_by_scalar = (CHUNKS - 1) * CHUNK - 1
         nc.scalar.activation(unread[:], table[:, last_by_scalar : last_by_scalar + 1], ACT.Gelu)

@@ -17,8 +17,9 @@ PAIRS = S // (PAIR * BLOCK)
 PAIRS_PER_CHUNK = BLOCKS_PER_CHUNK // PAIR
 AHEAD = 2 * PAIRS_PER_CHUNK
 STATS = 3
-PIECE = 512
+PIECE = 256
 PIECES = N // PIECE
+PIECES_IN_PSUM = 4
 OFFSETS_PER_COLUMN = 16
 
 FLOPS = 2 * D * M * N
@@ -33,7 +34,7 @@ def tile_intp_model_kernel(tc, seqs, ln_gain, ln_bias, lin_w, lin_b, offs, out):
         tc.tile_pool(name="turn", bufs=2 * PAIRS_PER_CHUNK) as turn,
         tc.tile_pool(name="done", bufs=PIECES) as done,
         tc.psum_pool(name="flip", bufs=3) as flip,
-        tc.psum_pool(name="proj", bufs=PIECES) as proj,
+        tc.psum_pool(name="proj", bufs=PIECES_IN_PSUM) as proj,
     ):
         gain = held.tile([D, 1], F32, name="gain")
         nc.scalar.dma_start(gain[:], ln_gain)

@@ -48,11 +48,11 @@ def tile_intp_model_kernel(tc, seqs, ln_gain, ln_bias, lin_w, lin_b, offs, out):
         unread = held.tile([P, 1], F32, name="unread")
         nc.scalar.activation(unread[:], eps[:], ACT.Abs_reciprocal_sqrt)
 
-        seqs_blocks = seqs.rearrange("(b p) d -> p b d", p=P)
+        seqs_chunks = seqs.rearrange("(c p b) d -> c p b d", p=P, b=BLOCKS_PER_CHUNK)
         raw_chunks = []
         for c in range(CHUNKS):
             raw = rows.tile([P, BLOCKS_PER_CHUNK, D], BF16, name="raw")
-            nc.sync.dma_start(raw[:], seqs_blocks[:, c * BLOCKS_PER_CHUNK : (c + 1) * BLOCKS_PER_CHUNK, :])
+            nc.sync.dma_start(raw[:], seqs_chunks[c])
             raw_chunks.append(raw)
         weights = held.tile([D, M], BF16, name="weights")
         nc.sync.dma_start(weights[:], lin_w)
@@ -88,11 +88,12 @@ def tile_intp_model_kernel(tc, seqs, ln_gain, ln_bias, lin_w, lin_b, offs, out):
                 nc.tensor.transpose(flipped[:, block * BLOCK : (block + 1) * BLOCK], normed[:, k, :], identity[:])
 
         def gain_and_bias(c, flipped):
-            columns = table[:, c * CHUNK : (c + 1) * CHUNK]
+            columns = table[:, c * CHUNK : (c + 1) * CHUNK].rearrange("d (p b) -> d p b", b=BLOCKS_PER_CHUNK)
+            by_station = flipped[:].rearrange("d (b p) -> d p b", b=BLOCKS_PER_CHUNK)
             if c < CHUNKS - 1:
-                nc.scalar.activation(columns, flipped[:], ACT.Identity, bias=shift[:], scale=gain[:])
+                nc.scalar.activation(columns, by_station, ACT.Identity, bias=shift[:], scale=gain[:])
             else:
-                nc.vector.tensor_scalar(columns, flipped[:], gain[:], shift[:], ALU.mult, ALU.add)
+                nc.vector.tensor_scalar(columns, by_station, gain[:], shift[:], ALU.mult, ALU.add)
 
         for q in range(AHEAD):
             statistics(q)

@@ -16,6 +16,7 @@ CHUNKS = S // CHUNK
 PAIRS = S // (PAIR * BLOCK)
 PAIRS_PER_CHUNK = BLOCKS_PER_CHUNK // PAIR
 AHEAD = 2 * PAIRS_PER_CHUNK
+CHUNKS_LEFT_TO_VECTOR = 2
 STATS = 3
 PIECE = 256
 PIECES = N // PIECE
@@ -90,7 +91,7 @@ def tile_intp_model_kernel(tc, seqs, ln_gain, ln_bias, lin_w, lin_b, offs, out):
         def gain_and_bias(c, flipped):
             columns = table[:, c * CHUNK : (c + 1) * CHUNK].rearrange("d (p b) -> d p b", b=BLOCKS_PER_CHUNK)
             by_station = flipped[:].rearrange("d (b p) -> d p b", b=BLOCKS_PER_CHUNK)
-            if c < CHUNKS - 1:
+            if c < CHUNKS - CHUNKS_LEFT_TO_VECTOR:
                 nc.scalar.activation(columns, by_station, ACT.Identity, bias=shift[:], scale=gain[:])
             else:
                 nc.vector.tensor_scalar(columns, by_station, gain[:], shift[:], ALU.mult, ALU.add)
@@ -105,7 +106,7 @@ def tile_intp_model_kernel(tc, seqs, ln_gain, ln_bias, lin_w, lin_b, offs, out):
                 normalise_and_turn(q, flipped)
             gain_and_bias(c, flipped)
 
-        last_by_scalar = (CHUNKS - 1) * CHUNK - 1
+        last_by_scalar = (CHUNKS - CHUNKS_LEFT_TO_VECTOR) * CHUNK - 1
         nc.scalar.activation(unread[:], table[:, last_by_scalar : last_by_scalar + 1], ACT.Gelu)
 
         columns_per_piece = PIECE // OFFSETS_PER_COLUMN

@@ -17,6 +17,7 @@ PAIRS = S // (PAIR * BLOCK)
 PAIRS_PER_CHUNK = BLOCKS_PER_CHUNK // PAIR
 AHEAD = 2 * PAIRS_PER_CHUNK
 CHUNKS_LEFT_TO_VECTOR = 2
+CHUNKS_BEFORE_GAIN_AND_BIAS = 2
 STATS = 3
 PIECE = 256
 PIECES = N // PIECE
@@ -37,11 +38,6 @@ def tile_intp_model_kernel(tc, seqs, ln_gain, ln_bias, lin_w, lin_b, offs, out):
         tc.psum_pool(name="flip", bufs=3) as flip,
         tc.psum_pool(name="proj", bufs=PIECES_IN_PSUM) as proj,
     ):
-        gain = held.tile([D, 1], F32, name="gain")
-        nc.scalar.dma_start(gain[:], ln_gain)
-        shift = held.tile([D, 1], F32, name="shift")
-        nc.scalar.dma_start(shift[:], ln_bias)
-
         identity = held.tile([P, P], F32, name="identity")
         make_identity(nc, identity[:])
         eps = held.tile([P, 1], F32, name="eps")
@@ -55,6 +51,11 @@ def tile_intp_model_kernel(tc, seqs, ln_gain, ln_bias, lin_w, lin_b, offs, out):
             raw = rows.tile([P, BLOCKS_PER_CHUNK, D], BF16, name="raw")
             nc.sync.dma_start(raw[:], seqs_chunks[c])
             raw_chunks.append(raw)
+            if c == CHUNKS_BEFORE_GAIN_AND_BIAS - 1:
+                gain = held.tile([D, 1], F32, name="gain")
+                nc.sync.dma_start(gain[:], ln_gain)
+                shift = held.tile([D, 1], F32, name="shift")
+                nc.sync.dma_start(shift[:], ln_bias)
         weights = held.tile([D, M], BF16, name="weights")
         nc.sync.dma_start(weights[:], lin_w)
         offsets = held.tile([P, N // OFFSETS_PER_COLUMN], U16, name="offsets")

@@ -17,7 +17,7 @@ PAIRS = S // (PAIR * BLOCK)
 PAIRS_PER_CHUNK = BLOCKS_PER_CHUNK // PAIR
 AHEAD = 2 * PAIRS_PER_CHUNK
 CHUNKS_LEFT_TO_VECTOR = 2
-CHUNKS_BEFORE_GAIN_AND_BIAS = 2
+CHUNKS_BEFORE_GAIN_AND_BIAS = 3
 STATS = 3
 PIECE = 256
 PIECES = N // PIECE

@@ -87,15 +87,15 @@ def tile_intp_model_kernel(tc, seqs, ln_gain, ln_bias, lin_w, lin_b, offs, out):
                     ALU.subtract, ALU.mult,
                 )
                 block = (q % PAIRS_PER_CHUNK) * PAIR + k
-                nc.tensor.transpose(flipped[:, block * BLOCK : (block + 1) * BLOCK], normed[:, k, :], identity[:])
+                every_fourth = flipped[:].rearrange("d (p b) -> d p b", b=BLOCKS_PER_CHUNK)[:, :, block]
+                nc.tensor.transpose(every_fourth, normed[:, k, :], identity[:])
 
         def gain_and_bias(c, flipped):
-            columns = table[:, c * CHUNK : (c + 1) * CHUNK].rearrange("d (p b) -> d p b", b=BLOCKS_PER_CHUNK)
-            by_station = flipped[:].rearrange("d (b p) -> d p b", b=BLOCKS_PER_CHUNK)
+            columns = table[:, c * CHUNK : (c + 1) * CHUNK]
             if c < CHUNKS - CHUNKS_LEFT_TO_VECTOR:
-                nc.scalar.activation(columns, by_station, ACT.Identity, bias=shift[:], scale=gain[:])
+                nc.scalar.activation(columns, flipped[:], ACT.Identity, bias=shift[:], scale=gain[:])
             else:
-                nc.vector.tensor_scalar(columns, by_station, gain[:], shift[:], ALU.mult, ALU.add)
+                nc.vector.tensor_scalar(columns, flipped[:], gain[:], shift[:], ALU.mult, ALU.add)
 
         for q in range(AHEAD):
             statistics(q)

@@ -20,7 +20,8 @@ CHUNKS_LEFT_TO_VECTOR = 2
 CHUNKS_BEFORE_GAIN_AND_BIAS = 3
 STATS = 3
 PIECE = 256
-PIECES = N // PIECE
+PIECE_WIDTHS = [PIECE // 2] * 2 + [PIECE] * (N // PIECE - 1)
+PIECES = len(PIECE_WIDTHS)
 PIECES_IN_PSUM = 4
 OFFSETS_PER_COLUMN = 16
 
@@ -110,11 +111,14 @@ def tile_intp_model_kernel(tc, seqs, ln_gain, ln_bias, lin_w, lin_b, offs, out):
         last_by_scalar = (CHUNKS - CHUNKS_LEFT_TO_VECTOR) * CHUNK - 1
         nc.scalar.activation(unread[:], table[:, last_by_scalar : last_by_scalar + 1], ACT.Gelu)
 
-        columns_per_piece = PIECE // OFFSETS_PER_COLUMN
-        for j in range(PIECES):
-            picked = table[:].indirect(offsets[:, j * columns_per_piece : (j + 1) * columns_per_piece])
+        first = 0
+        for width in PIECE_WIDTHS:
+            picked = table[:].indirect(
+                offsets[:, first // OFFSETS_PER_COLUMN : (first + width) // OFFSETS_PER_COLUMN]
+            )
             product = proj.tile([M, PIECE], F32, name="product")
-            nc.tensor.matmul(product[:], weights[:], picked, start=True, stop=True)
+            nc.tensor.matmul(product[:, :width], weights[:], picked, start=True, stop=True)
             result = done.tile([M, PIECE], F32, name="result")
-            nc.scalar.activation(result[:], product[:], ACT.Gelu, bias=out_bias[:])
-            nc.sync.dma_start(out[:, j * PIECE : (j + 1) * PIECE], result[:])
+            nc.scalar.activation(result[:, :width], product[:, :width], ACT.Gelu, bias=out_bias[:])
+            nc.sync.dma_start(out[:, first : first + width], result[:, :width])
+            first += width

@@ -34,9 +34,9 @@ def tile_intp_model_kernel(tc, seqs, ln_gain, ln_bias, lin_w, lin_b, offs, out):
         tc.tile_pool(name="held", bufs=1) as held,
         tc.tile_pool(name="rows", bufs=CHUNKS) as rows,
         tc.tile_pool(name="ahead", bufs=AHEAD + 2) as ahead,
-        tc.tile_pool(name="turn", bufs=2 * PAIRS_PER_CHUNK) as turn,
+        tc.tile_pool(name="turn", bufs=2 * PAIRS_PER_CHUNK + 1) as turn,
         tc.tile_pool(name="done", bufs=PIECES) as done,
-        tc.psum_pool(name="flip", bufs=3) as flip,
+        tc.psum_pool(name="flip", bufs=4) as flip,
         tc.psum_pool(name="proj", bufs=PIECES_IN_PSUM) as proj,
     ):
         identity = held.tile([P, P], F32, name="identity")

@@ -15,7 +15,7 @@ CHUNK = BLOCKS_PER_CHUNK * BLOCK
 CHUNKS = S // CHUNK
 PAIRS = S // (PAIR * BLOCK)
 PAIRS_PER_CHUNK = BLOCKS_PER_CHUNK // PAIR
-AHEAD = 2 * PAIRS_PER_CHUNK
+AHEAD = 2 * PAIRS_PER_CHUNK + 1
 CHUNKS_LEFT_TO_VECTOR = 2
 CHUNKS_BEFORE_GAIN_AND_BIAS = 3
 STATS = 3

import concourse.mybir as mybir
from concourse.masks import make_identity

BF16, F32, U16 = mybir.dt.bfloat16, mybir.dt.float32, mybir.dt.uint16
ACT = mybir.ActivationFunctionType
ALU = mybir.AluOpType

P = 128
S, D, M, N = 4096, 128, 128, 2048
EPS = 1e-6
BLOCK = P
PAIR = 2
BLOCKS_PER_CHUNK = 4
CHUNK = BLOCKS_PER_CHUNK * BLOCK
CHUNKS = S // CHUNK
PAIRS = S // (PAIR * BLOCK)
PAIRS_PER_CHUNK = BLOCKS_PER_CHUNK // PAIR
AHEAD = 2 * PAIRS_PER_CHUNK + 1
CHUNKS_LEFT_TO_VECTOR = 2
CHUNKS_BEFORE_GAIN_AND_BIAS = 3
STATS = 3
PIECE = 256
PIECE_WIDTHS = [PIECE // 2] * 2 + [PIECE] * (N // PIECE - 1)
PIECES = len(PIECE_WIDTHS)
PIECES_IN_PSUM = 4
OFFSETS_PER_COLUMN = 16

FLOPS = 2 * D * M * N


def tile_intp_model_kernel(tc, seqs, ln_gain, ln_bias, lin_w, lin_b, offs, out):
    nc = tc.nc
    with (
        tc.tile_pool(name="held", bufs=1) as held,
        tc.tile_pool(name="rows", bufs=CHUNKS) as rows,
        tc.tile_pool(name="ahead", bufs=AHEAD + 2) as ahead,
        tc.tile_pool(name="turn", bufs=2 * PAIRS_PER_CHUNK + 1) as turn,
        tc.tile_pool(name="done", bufs=PIECES) as done,
        tc.psum_pool(name="flip", bufs=4) as flip,
        tc.psum_pool(name="proj", bufs=PIECES_IN_PSUM) as proj,
    ):
        identity = held.tile([P, P], F32, name="identity")
        make_identity(nc, identity[:])
        eps = held.tile([P, 1], F32, name="eps")
        nc.vector.memset(eps[:], EPS)
        unread = held.tile([P, 1], F32, name="unread")
        nc.scalar.activation(unread[:], eps[:], ACT.Abs_reciprocal_sqrt)

        seqs_chunks = seqs.rearrange("(c p b) d -> c p b d", p=P, b=BLOCKS_PER_CHUNK)
        raw_chunks = []
        for c in range(CHUNKS):
            raw = rows.tile([P, BLOCKS_PER_CHUNK, D], BF16, name="raw")
            nc.sync.dma_start(raw[:], seqs_chunks[c])
            raw_chunks.append(raw)
            if c == CHUNKS_BEFORE_GAIN_AND_BIAS - 1:
                gain = held.tile([D, 1], F32, name="gain")
                nc.sync.dma_start(gain[:], ln_gain)
                shift = held.tile([D, 1], F32, name="shift")
                nc.sync.dma_start(shift[:], ln_bias)
        weights = held.tile([D, M], BF16, name="weights")
        nc.sync.dma_start(weights[:], lin_w)
        offsets = held.tile([P, N // OFFSETS_PER_COLUMN], U16, name="offsets")
        nc.sync.dma_start(offsets[:], offs)
        out_bias = held.tile([M, 1], F32, name="out_bias")
        nc.sync.dma_start(out_bias[:], lin_b)

        table = held.tile([D, S], BF16, name="table")

        def raw_pair(q):
            first = (q % PAIRS_PER_CHUNK) * PAIR
            return raw_chunks[q // PAIRS_PER_CHUNK][:, first : first + PAIR, :]

        means, rstds = {}, {}

        def statistics(q):
            stats = ahead.tile([P, PAIR, STATS], F32, name="stats")
            nc.vector.bn_stats(stats[:].rearrange("p k t -> p (k t)"), raw_pair(q).rearrange("p k d -> p d k"))
            count_times_var = stats[:, :, 2]
            rstd = ahead.tile([P, PAIR], F32, name="rstd")
            nc.scalar.activation(rstd[:], count_times_var, ACT.Abs_reciprocal_sqrt, bias=eps[:], scale=1.0 / D)
            means[q], rstds[q] = stats[:, :, 1], rstd

        def normalise_and_turn(q, flipped):
            normed = turn.tile([P, PAIR, D], F32, name="normed")
            for k in range(PAIR):
                nc.vector.tensor_scalar(
                    normed[:, k, :], raw_pair(q)[:, k, :], means[q][:, k : k + 1], rstds[q][:, k : k + 1],
                    ALU.subtract, ALU.mult,
                )
                block = (q % PAIRS_PER_CHUNK) * PAIR + k
                every_fourth = flipped[:].rearrange("d (p b) -> d p b", b=BLOCKS_PER_CHUNK)[:, :, block]
                nc.tensor.transpose(every_fourth, normed[:, k, :], identity[:])

        def gain_and_bias(c, flipped):
            columns = table[:, c * CHUNK : (c + 1) * CHUNK]
            if c < CHUNKS - CHUNKS_LEFT_TO_VECTOR:
                nc.scalar.activation(columns, flipped[:], ACT.Identity, bias=shift[:], scale=gain[:])
            else:
                nc.vector.tensor_scalar(columns, flipped[:], gain[:], shift[:], ALU.mult, ALU.add)

        for q in range(AHEAD):
            statistics(q)
        for c in range(CHUNKS):
            flipped = flip.tile([D, CHUNK], F32, name="flipped")
            for q in range(c * PAIRS_PER_CHUNK, (c + 1) * PAIRS_PER_CHUNK):
                if q + AHEAD < PAIRS:
                    statistics(q + AHEAD)
                normalise_and_turn(q, flipped)
            gain_and_bias(c, flipped)

        last_by_scalar = (CHUNKS - CHUNKS_LEFT_TO_VECTOR) * CHUNK - 1
        nc.scalar.activation(unread[:], table[:, last_by_scalar : last_by_scalar + 1], ACT.Gelu)

        first = 0
        for width in PIECE_WIDTHS:
            picked = table[:].indirect(
                offsets[:, first // OFFSETS_PER_COLUMN : (first + width) // OFFSETS_PER_COLUMN]
            )
            product = proj.tile([M, PIECE], F32, name="product")
            nc.tensor.matmul(product[:, :width], weights[:], picked, start=True, stop=True)
            result = done.tile([M, PIECE], F32, name="result")
            nc.scalar.activation(result[:, :width], product[:, :width], ACT.Gelu, bias=out_bias[:])
            nc.sync.dma_start(out[:, first : first + width], result[:, :width])
            first += width
